import numpy as np
import ml_dtypes


def mxq(x, axis, fmt="e4m3"):
    dtype, down = {"e4m3": (ml_dtypes.float8_e4m3fn, 7), "e5m2": (ml_dtypes.float8_e5m2, 14)}[fmt]
    v = np.moveaxis(np.asarray(x, np.float32).astype(ml_dtypes.bfloat16).astype(np.float64), axis, -1)
    blocks = v.reshape(v.shape[:-1] + (-1, 32))
    amax = np.abs(blocks).max(-1, keepdims=True)
    byte = np.maximum(np.where(amax > 0, np.frexp(amax)[1] - 1 + 127, 0) - down, 1)
    scale = np.exp2(byte - 127.0)
    codes = (blocks / scale).astype(np.float32).astype(dtype).astype(np.float64)
    return np.moveaxis((codes * scale).reshape(v.shape), -1, axis)


WIDE = False


def mx_kscale(k):
    if not WIDE:
        return np.ones(k)
    levels = np.array([18, -18])
    if k % 512:
        return np.exp2(np.random.permutation(np.resize(levels, k // 32))).repeat(32)
    a = np.empty((k // 512, 16))
    for p in range(k // 512):
        a[p, :8] = np.random.permutation(np.resize(levels, 8))
        for g in range(8):
            far = levels[np.abs(levels - a[p, g]) >= 10]
            a[p, g + 8] = far[np.random.randint(len(far))]
    return np.exp2(a.ravel()).repeat(32)


BF16 = ml_dtypes.bfloat16


def bf(x):
    return np.asarray(x, np.float32).astype(BF16)


def f64(x):
    return np.asarray(x).astype(np.float64)


N, D, O = 1024, 512, 512
LEAKY_SLOPE = 0.01
P_EDGE = 0.25
ZS = np.sqrt(N) / 8.0
GS = 16.0


def setup_inputs():
    u = mx_kscale(N)
    v = mx_kscale(O)
    s = mx_kscale(N)
    edges = np.random.random((N, N)) < P_EDGE
    a0 = bf((0.1 + 0.9 * np.random.random((N, N))) * edges + np.eye(N))
    h0 = bf(np.random.standard_normal((N, D)))
    w0 = bf(np.random.standard_normal((D, O)) * ZS / np.sqrt(D))
    bout = bf(0.1 * np.random.standard_normal(O) - 0.2)
    g = bf(np.random.standard_normal((N, O)) * np.exp2(np.random.randint(-6, 1, (N, 1))) * GS * u[:, None] * v[None, :])
    A = f64(a0)
    d = np.power(A.sum(axis=1), -0.5)
    A_hat = A * d[:, None] * d[None, :]
    y = A_hat @ (f64(h0) @ f64(w0) + f64(bout))
    return {"A1": bf(A / u[:, None] / s[None, :]),
            "Hn": bf(f64(h0) * s[:, None]),
            "Wout": bf(f64(w0) / v[None, :]),
            "bout": bout,
            "d": np.asarray(d, np.float32),
            "y": np.asarray(y, np.float32),
            "grad_out": g}


def reference(A1, Hn, Wout, bout, d, y, grad_out):
    df = f64(d)
    slope = np.where(f64(y) >= 0, 1.0, LEAKY_SLOPE)
    dz2 = f64(grad_out) * slope * df[:, None]
    dh = mxq(f64(A1), 0, "e4m3").T @ mxq(dz2, 0, "e5m2")
    dz1 = dh * df[:, None]
    dHn = mxq(dz1, 1, "e5m2") @ mxq(f64(Wout), 1, "e4m3").T
    dWout = mxq(f64(Hn), 0, "e4m3").T @ mxq(dz1, 0, "e5m2")
    return dHn, dWout

@@ -1,0 +1,231 @@
+from contextlib import ExitStack
+
+import concourse.mybir as mybir
+from concourse.masks import make_identity
+
+N, D, O = 1024, 512, 512
+SLOPE = 0.01
+FLOPS = 2 * (N * N * O + 2 * N * O * D)
+BYTES = 2 * (N * N + N * D + D * O + N * O) + 4 * (N + N * O) + 4 * (N * D + D * O)
+
+F32 = mybir.dt.float32
+BF16 = mybir.dt.bfloat16
+U32 = mybir.dt.uint32
+U8 = mybir.dt.uint8
+E4 = mybir.dt.float8_e4m3fn_x4
+E5 = mybir.dt.float8_e5m2_x4
+ALU = mybir.AluOpType
+ACT = mybir.ActivationFunctionType
+
+P = 128
+ORDER = """Ld Lg0 Ly0a LA00 Ly0b Lg1 Ly1a LA10 Ly1b LW LA01 LA11 LH0 LH1 Id
+gd0a gd0b sl0a tt0a iA00@S sl0b tt0b gd1a gd1b qA00 sl1a qz0 tt1a sl1b tt1b iA10@S
+d000 d001 tWa tWb d002 d003 cWa@S jA01a@S qA10 qz1  cWb@S
+d100 d101 d102 d103 jA01b@V iA11@V Z00@S qA01 Z01@S qA11 tF0a d010 d011  Z02@S Z03@S d012 d013 tF0b d110 d111
+ d112 d113 qW cF0a@S  cF0b@S qF0a iT0@V  qF0b Z10@S Z11@S
+o00 o01  o02 o03 tF1a Z12@S Z13@S qT0 iH0@V E00@V S00 qH0 tF1b cF1a@S iT1@V  cF1b@S E01@S S01  qF1a qT1 qF1b E02@S S02  E03@S S03
+o10 o11 o12 o13 w00 w10  iH1@V iH2@V qH1 E10@S S10 E11@S S11 qH2 w01 w11 iH3@V  E12@S S12 E13@S S13 qH3 w02 w12 w03 w13 G0@V R0
+ G1@S R1  G2@V R2 G3@S R3""".split()
+BANK = {"dh00": 0, "dh01": 1, "dh02": 2, "dh03": 3, "tWa": 6, "tWb": 7, "dh10": 4, "dh11": 5, "dh12": 6, "dh13": 7,
+        "tF0a": 0, "tF0b": 1, "o00": 2, "o01": 3, "o02": 0, "o03": 1, "tF1a": 4, "tF1b": 5, "o10": 6, "o11": 7, "o12": 2, "o13": 4,
+        "w0": 3, "w1": 0, "w2": 1, "w3": 6}
+
+
+def tile_gcnlayer_pb_v_kernel(tc, A1, Hn, Wout, bout, d, y, grad_out, out_0, out_1):
+    nc = tc.nc
+    with ExitStack() as ctx:
+        sb = ctx.enter_context(tc.tile_pool(name="sb", bufs=1))
+        ps = ctx.enter_context(tc.psum_pool(name="ps", bufs=1))
+        ctx.enter_context(tc.manual_schedule())
+
+        def sbt(name, shape, dtype):
+            return sb.tile(shape, dtype, name=name, tag=name, align_bytes=64)
+
+        banks = {}
+
+        def bank(name):
+            banks[name] = ps.tile([P, 512], F32, name="ps_" + name, tag="bank%d" % BANK[name])
+            return banks[name]
+
+        def copy(eng, out, in_):
+            if eng == "V":
+                nc.vector.tensor_copy(out=out, in_=in_)
+            else:
+                nc.scalar.copy(out=out, in_=in_)
+
+        two = (0, 1)
+        four = (0, 1, 2, 3)
+        d_sb = sbt("d_sb", [P, 2, 4], F32)
+        g_raw = [sbt("g_raw%d" % g, [P, 4, 512], BF16) for g in two]
+        y_raw = [[sbt("y_raw%d%d" % (g, a), [P, 4, 256], F32) for a in two] for g in two]
+        slope = [[sbt("slope%d%d" % (g, a), [P, 4, 256], F32) for a in two] for g in two]
+        gd = [[sbt("gd%d%d" % (g, a), [P, 4, 256], F32) for a in two] for g in two]
+        z_il = [sbt("z_il%d" % g, [P, 2048], BF16) for g in two]
+        z_c = [sbt("z_c%d" % g, [P, 512], U32) for g in two]
+        z_s = [sbt("z_s%d" % g, [P, 512], U8) for g in two]
+        a_raw = [[sbt("a_raw%d%d" % (g, h), [P, 4, 512], BF16) for h in two] for g in two]
+        a_il = [[sbt("a_il%d%d" % (g, h), [P, 2048], BF16) for h in two] for g in two]
+        a_c = [[sbt("a_c%d%d" % (g, h), [P, 512], U32) for h in two] for g in two]
+        a_s = [[sbt("a_s%d%d" % (g, h), [P, 512], U8) for h in two] for g in two]
+        w_raw = sbt("w_raw", [P, 2048], BF16)
+        w_il = sbt("w_il", [P, 2048], BF16)
+        w_c = sbt("w_c", [P, 512], U32)
+        w_s = sbt("w_s", [P, 512], U8)
+        h_raw = sbt("h_raw", [P, 2, 4, 512], BF16)
+        h_il = [sbt("h_il%d" % a, [P, 1024], BF16) for a in four]
+        h_c = [sbt("h_c%d" % a, [P, 256], U32) for a in four]
+        h_s = [sbt("h_s%d" % a, [P, 256], U8) for a in four]
+        dz1 = [sbt("dz1_%d" % h, [P, 2048], BF16) for h in two]
+        f_il = [[sbt("f_il%d%d" % (h, k), [P, 1024], BF16) for k in two] for h in two]
+        f_c = [[sbt("f_c%d%d" % (h, k), [P, 256], U32) for k in two] for h in two]
+        f_s = [[sbt("f_s%d%d" % (h, k), [P, 256], U8) for k in two] for h in two]
+        t_il = [sbt("t_il%d" % h, [P, 2048], BF16) for h in two]
+        t_c = [sbt("t_c%d" % h, [P, 512], U32) for h in two]
+        t_s = [sbt("t_s%d" % h, [P, 512], U8) for h in two]
+        o0 = [[sbt("o0_%d%d" % (h, t), [P, 512], F32) for t in four] for h in two]
+        o1 = [sbt("o1_%d" % a, [P, 512], F32) for a in four]
+        ident_g = sbt("ident_g", [P, P], F32)
+        ident = sbt("ident", [P, P], F32)
+
+        def rows(src, g):
+            return src[512 * g : 512 * (g + 1), :].rearrange("(p j) w -> p j w", j=4)
+
+        def quant(codes, scales, src, fmt):
+            nc.vector.quantize_mx(out=codes.bitcast(fmt), scales=scales, in_=src)
+
+        def mm(out, lc, ls, lf, rc, rs, rf, start, stop):
+            nc.tensor.matmul_mx(out=out, lhsT=lc.bitcast(lf), lhsT_scale=ls, rhs=rc.bitcast(rf), rhs_scale=rs, start=start, stop=stop)
+
+        def a_views(g, h):
+            src = a_raw[g][h][:].rearrange("p j (mm m t) -> p mm t j m", m=2, t=4)
+            return src
+
+        def step(name, eng):
+            kind = name[:2]
+            if name == "Id":
+                make_identity(nc, ident_g[:])
+                nc.scalar.activation(out=ident[:], in_=ident_g[:], func=ACT.Copy)
+            elif name == "Ld":
+                nc.scalar.dma_start(out=d_sb[:], in_=d.rearrange("(g p j) -> p g j", g=2, j=4))
+            elif kind == "Lg":
+                g = int(name[2])
+                nc.sync.dma_start(out=g_raw[g][:], in_=rows(grad_out, g))
+            elif kind == "Ly":
+                g, a = int(name[2]), "ab".index(name[3])
+                nc.sync.dma_start(out=y_raw[g][a][:], in_=rows(y, g)[:, :, 256 * a : 256 * (a + 1)])
+            elif kind == "LA":
+                g, h = int(name[2]), int(name[3])
+                nc.sync.dma_start(out=a_raw[g][h][:], in_=rows(A1, g)[:, :, 512 * h : 512 * (h + 1)])
+            elif kind == "LW":
+                nc.sync.dma_start(out=w_raw[:], in_=Wout.rearrange("(p a) o -> p (a o)", a=4))
+            elif kind == "LH":
+                h = int(name[2])
+                nc.sync.dma_start(out=h_raw[:, h], in_=rows(Hn, h))
+            elif kind == "gd":
+                g, a = int(name[2]), "ab".index(name[3])
+                for j in four:
+                    nc.scalar.activation(out=gd[g][a][:, j, :], in_=g_raw[g][:, j, 256 * a : 256 * (a + 1)], func=ACT.Copy, scale=d_sb[:, g, j : j + 1])
+            elif kind == "sl":
+                g, a = int(name[2]), "ab".index(name[3])
+                nc.vector.tensor_scalar(out=slope[g][a][:].rearrange("p j w -> p (j w)"), in0=y_raw[g][a][:].rearrange("p j w -> p (j w)"), scalar1=0.0, scalar2=SLOPE, op0=ALU.is_ge, op1=ALU.max)
+            elif kind == "tt":
+                g, a = int(name[2]), "ab".index(name[3])
+                nc.vector.tensor_tensor(
+                    out=z_il[g][:, 1024 * a : 1024 * (a + 1)].rearrange("p (c i j) -> p c j i", i=4, j=4),
+                    in0=gd[g][a][:].rearrange("p j (c i) -> p c j i", i=4),
+                    in1=slope[g][a][:].rearrange("p j (c i) -> p c j i", i=4),
+                    op=ALU.mult,
+                )
+            elif kind == "qz":
+                g = int(name[2])
+                quant(z_c[g][:], z_s[g][:], z_il[g][:], E5)
+            elif kind == "iA":
+                g, h = int(name[2]), int(name[3])
+                copy(eng, a_il[g][h][:].rearrange("p (t mm m j) -> p mm t j m", t=4, m=2, j=4), a_views(g, h))
+            elif kind == "jA":
+                g, h, k = int(name[2]), int(name[3]), "ab".index(name[4])
+                copy(eng, a_il[g][h][:, 1024 * k : 1024 * (k + 1)].rearrange("p (t mm m j) -> p mm t j m", t=2, m=2, j=4), a_views(g, h)[:, :, 2 * k : 2 * k + 2])
+            elif kind == "qA":
+                g, h = int(name[2]), int(name[3])
+                quant(a_c[g][h][:], a_s[g][h][:], a_il[g][h][:], E4)
+            elif kind == "tW":
+                k = "ab".index(name[2])
+                b = bank(name)
+                words = w_raw[:].bitcast(F32)
+                for a2 in two:
+                    for u in two:
+                        a = 2 * k + a2
+                        nc.tensor.transpose(b[:, 128 * (2 * a2 + u) : 128 * (2 * a2 + u + 1)], words[:, 256 * a + u : 256 * (a + 1) : 2], ident[:])
+            elif kind == "cW":
+                k = "ab".index(name[2])
+                copy(eng, w_il[:].bitcast(F32).rearrange("q (p a u) -> q p a u", a=4, u=2)[:, :, 2 * k : 2 * k + 2, :], banks["tW" + name[2]][:].rearrange("q (a u p) -> q p a u", a=2, u=2))
+            elif name == "qW":
+                quant(w_c[:], w_s[:], w_il[:], E4)
+            elif name[0] == "d":
+                g, h, t = int(name[1]), int(name[2]), int(name[3])
+                key = "dh%d%d" % (h, t)
+                b = bank(key) if g == 0 else banks[key]
+                cols = slice(128 * t, 128 * (t + 1))
+                mm(b[:], a_c[g][h][:, cols], a_s[g][h][:, cols], E4, z_c[g][:], z_s[g][:], E5, g == 0, g == 1)
+            elif name[0] == "Z":
+                h, t = int(name[1]), int(name[2])
+                dst = dz1[h][:, 512 * t : 512 * (t + 1)].rearrange("p (u m e) -> p u m e", u=2, e=2)
+                src = banks["dh%d%d" % (h, t)][:].rearrange("p (m u e) -> p u m e", u=2, e=2)
+                if eng == "S":
+                    nc.scalar.activation(out=dst, in_=src, func=ACT.Copy, scale=d_sb[:, h, t : t + 1])
+                else:
+                    nc.vector.tensor_scalar(out=dst, in0=src, scalar1=d_sb[:, h, t : t + 1], scalar2=None, op0=ALU.mult)
+            elif kind == "tF":
+                h, k = int(name[2]), "ab".index(name[3])
+                b = bank(name)
+                for t2 in two:
+                    for u in two:
+                        c0 = 512 * (2 * k + t2) + 256 * u
+                        nc.tensor.transpose(b[:, 128 * (2 * t2 + u) : 128 * (2 * t2 + u + 1)], dz1[h][:, c0 : c0 + 256].bitcast(F32), ident[:])
+            elif kind == "cF":
+                h, k = int(name[2]), "ab".index(name[3])
+                copy(eng, f_il[h][k][:].bitcast(F32).rearrange("p (t r u) -> p t r u", t=2, u=2), banks["tF" + name[2:]][:].rearrange("p (t u r) -> p t r u", t=2, u=2))
+            elif kind == "qF":
+                h, k = int(name[2]), "ab".index(name[3])
+                quant(f_c[h][k][:], f_s[h][k][:], f_il[h][k][:], E5)
+            elif kind == "iT":
+                h = int(name[2])
+                copy(eng, t_il[h][:].rearrange("p (c i t) -> p c t i", i=4, t=4), dz1[h][:].rearrange("p (t c i) -> p c t i", i=4, t=4))
+            elif kind == "qT":
+                h = int(name[2])
+                quant(t_c[h][:], t_s[h][:], t_il[h][:], E5)
+            elif kind == "iH":
+                a = int(name[2])
+                copy(eng, h_il[a][:].rearrange("p (h c i j) -> p h c j i", h=2, i=4, j=4), h_raw[:, :, :, 128 * a : 128 * (a + 1)].rearrange("p h j (c i) -> p h c j i", i=4))
+            elif kind == "qH":
+                a = int(name[2])
+                quant(h_c[a][:], h_s[a][:], h_il[a][:], E4)
+            elif name[0] == "o":
+                h, t = int(name[1]), int(name[2])
+                b = bank(name)
+                cols = slice(128 * (t % 2), 128 * (t % 2 + 1))
+                mm(b[:], f_c[h][t // 2][:, cols], f_s[h][t // 2][:, cols], E5, w_c[:], w_s[:], E4, True, True)
+            elif name[0] == "w":
+                h, a = int(name[1]), int(name[2])
+                key = "w%d" % a
+                b = bank(key) if h == 0 else banks[key]
+                cols = slice(128 * h, 128 * (h + 1))
+                mm(b[:], h_c[a][:, cols], h_s[a][:, cols], E4, t_c[h][:], t_s[h][:], E5, h == 0, h == 1)
+            elif name[0] == "E":
+                h, t = int(name[1]), int(name[2])
+                copy(eng, o0[h][t][:], banks["o%d%d" % (h, t)][:])
+            elif name[0] == "S":
+                h, t = int(name[1]), int(name[2])
+                nc.sync.dma_start(out=out_0[512 * h : 512 * (h + 1), :].rearrange("(p t) w -> p t w", t=4)[:, t, :], in_=o0[h][t][:])
+            elif name[0] == "G":
+                a = int(name[1])
+                copy(eng, o1[a][:].rearrange("p (m u e) -> p m u e", u=2, e=2), banks["w%d" % a][:].rearrange("p (u m e) -> p m u e", u=2, e=2))
+            elif name[0] == "R":
+                a = int(name[1])
+                nc.sync.dma_start(out=out_1[128 * a : 128 * (a + 1), :], in_=o1[a][:])
+            else:
+                raise ValueError(name)
+
+        for item in ORDER:
+            parts = item.split("@")
+            step(parts[0], parts[1] if len(parts) > 1 else "")

@@ -18,17 +18,15 @@ ALU = mybir.AluOpType
 ACT = mybir.ActivationFunctionType
 
 P = 128
-ORDER = """Ld Lg0 Ly0a LA00 Ly0b Lg1 Ly1a LA10 Ly1b LW LA01 LA11 LH0 LH1 Id
-gd0a gd0b sl0a tt0a iA00@S sl0b tt0b gd1a gd1b qA00 sl1a qz0 tt1a sl1b tt1b iA10@S
-d000 d001 tWa tWb d002 d003 cWa@S jA01a@S qA10 qz1  cWb@S
-d100 d101 d102 d103 jA01b@V iA11@V Z00@S qA01 Z01@S qA11 tF0a d010 d011  Z02@S Z03@S d012 d013 tF0b d110 d111
- d112 d113 qW cF0a@S  cF0b@S qF0a iT0@V  qF0b Z10@S Z11@S
-o00 o01  o02 o03 tF1a Z12@S Z13@S qT0 iH0@V E00@V S00 qH0 tF1b cF1a@S iT1@V  cF1b@S E01@S S01  qF1a qT1 qF1b E02@S S02  E03@S S03
-o10 o11 o12 o13 w00 w10  iH1@V iH2@V qH1 E10@S S10 E11@S S11 qH2 w01 w11 iH3@V  E12@S S12 E13@S S13 qH3 w02 w12 w03 w13 G0@V R0
- G1@S R1  G2@V R2 G3@S R3""".split()
-BANK = {"dh00": 0, "dh01": 1, "dh02": 2, "dh03": 3, "tWa": 6, "tWb": 7, "dh10": 4, "dh11": 5, "dh12": 6, "dh13": 7,
-        "tF0a": 0, "tF0b": 1, "o00": 2, "o01": 3, "o02": 0, "o03": 1, "tF1a": 4, "tF1b": 5, "o10": 6, "o11": 7, "o12": 2, "o13": 4,
-        "w0": 3, "w1": 0, "w2": 1, "w3": 6}
+ORDER = """Ld Lg0 Ly0a LA00 Ly0b Lg1 Ly1a LA10 Ly1b LA01 LW LA11 LH0 LH1 Id
+gd0a gd0b sl0a tt0a iA00@S sl0b qz0a tt0b gd1a gd1b qA00 sl1a qz0b tt1a sl1b qz1a tt1b iA10@S 
+d000 d001 d002 d003 tWa tWb iA01@S cWa@S cWb@S qA10 qz1b  
+d100 d101 d102 d103 iA11@V Z00@S qA01 Z01@S qA11 d010 d110 tF0a  Z02@S Z03@S d011 d111 tF0b d012 d112 
+qW iH0@V iH1@V qH0 cF0a@S qH1 qF0a d013 d113 o00 o01 iT0@V Z10@S cF0b@S Z11@S qF0b qT0
+ tF1a o02 o03  Z12@S Z13@S E00@V S00 E01@V S01  tF1b w00 w01 cF1a@S qF1a o10 o11 iT1@V E02@S S02 cF1b@S  qF1b qT1 E03@S S03 
+ o12 o13 w10 w11  iH2@V iH3@V qH2 E10@S S10 E11@S S11 qH3 w02 w12 w03 w13 E12@S S12  E13@S S13 G0@S R0 G1@V R1 
+ G2@S R2 G3@V R3""".split()
+BANK = {"dh00":0,"dh01":1,"dh02":2,"dh03":3,"dh10":4,"dh11":5,"tWa":6,"tWb":7,"dh12":6,"dh13":7,"tF0a":0,"tF0b":1,"o00":2,"o01":3,"o02":0,"o03":1,"tF1a":4,"tF1b":5,"w0":6,"w1":7,"o10":2,"o11":3,"o12":4,"o13":0,"w2":5,"w3":1}
 
 
 def tile_gcnlayer_pb_v_kernel(tc, A1, Hn, Wout, bout, d, y, grad_out, out_0, out_1):
@@ -137,8 +135,8 @@ def tile_gcnlayer_pb_v_kernel(tc, A1, Hn, Wout, bout, d, y, grad_out, out_0, out
                     op=ALU.mult,
                 )
             elif kind == "qz":
-                g = int(name[2])
-                quant(z_c[g][:], z_s[g][:], z_il[g][:], E5)
+                g, a = int(name[2]), "ab".index(name[3])
+                quant(z_c[g][:, 256 * a : 256 * (a + 1)], z_s[g][:, 256 * a : 256 * (a + 1)], z_il[g][:, 1024 * a : 1024 * (a + 1)], E5)
             elif kind == "iA":
                 g, h = int(name[2]), int(name[3])
                 copy(eng, a_il[g][h][:].rearrange("p (t mm m j) -> p mm t j m", t=4, m=2, j=4), a_views(g, h))

@@ -18,13 +18,12 @@ ALU = mybir.AluOpType
 ACT = mybir.ActivationFunctionType
 
 P = 128
-ORDER = """Ld Lg0 Ly0a LA00 Ly0b Lg1 Ly1a LA10 Ly1b LA01 LW LA11 LH0 LH1 Id
-gd0a gd0b sl0a tt0a iA00@S sl0b qz0a tt0b gd1a gd1b qA00 sl1a qz0b tt1a sl1b qz1a tt1b iA10@S 
-d000 d001 d002 d003 tWa tWb iA01@S cWa@S cWb@S qA10 qz1b  
-d100 d101 d102 d103 iA11@V Z00@S qA01 Z01@S qA11 d010 d110 tF0a  Z02@S Z03@S d011 d111 tF0b d012 d112 
-qW iH0@V iH1@V qH0 cF0a@S qH1 qF0a d013 d113 o00 o01 iT0@V Z10@S cF0b@S Z11@S qF0b qT0
+ORDER = """Ld Lg0 Ly0p Ly0q Lg1 LA0 Ly1p Ly1q LA1 LW LH0 LH1 Id
+gd0a gd0b sl0a sl0b tt0a tt0b qz0a gd1a gd1b jA00a@S qz0b jA00b@V iA01@S sl1a qA00 sl1b tt1a tt1b jA10a@S qz1a jA10b@V qz1b qA10
+d000 d001 d002 d003 tWa tWb jA11a@S cWa@S cWb@S d100 d101 d102 d103 jA11b@V qA01 qA11 Z00@S  Z01@S d010 d110 tF0a Z02@S Z03@S d011 d111 tF0b d012 d112 
+qW iH0@V iH1@V qH0 cF0a@S qH1 iH2@V qF0a d013 d113 o00 o01 iT0@V Z10@S cF0b@S Z11@S qF0b qT0
  tF1a o02 o03  Z12@S Z13@S E00@V S00 E01@V S01  tF1b w00 w01 cF1a@S qF1a o10 o11 iT1@V E02@S S02 cF1b@S  qF1b qT1 E03@S S03 
- o12 o13 w10 w11  iH2@V iH3@V qH2 E10@S S10 E11@S S11 qH3 w02 w12 w03 w13 E12@S S12  E13@S S13 G0@S R0 G1@V R1 
+ o12 o13 w10 w11  iH3@V qH2 E10@S S10 E11@S S11 qH3 w02 w12 w03 w13 E12@S S12  E13@S S13 G0@S R0 G1@V R1 
  G2@S R2 G3@V R3""".split()
 BANK = {"dh00":0,"dh01":1,"dh02":2,"dh03":3,"dh10":4,"dh11":5,"tWa":6,"tWb":7,"dh12":6,"dh13":7,"tF0a":0,"tF0b":1,"o00":2,"o01":3,"o02":0,"o03":1,"tF1a":4,"tF1b":5,"w0":6,"w1":7,"o10":2,"o11":3,"o12":4,"o13":0,"w2":5,"w3":1}
 
@@ -53,15 +52,15 @@ def tile_gcnlayer_pb_v_kernel(tc, A1, Hn, Wout, bout, d, y, grad_out, out_0, out
 
         two = (0, 1)
         four = (0, 1, 2, 3)
-        d_sb = sbt("d_sb", [P, 2, 4], F32)
+        d_sb = [sbt("d_sb%d" % g, [P, 4], F32) for g in two]
         g_raw = [sbt("g_raw%d" % g, [P, 4, 512], BF16) for g in two]
-        y_raw = [[sbt("y_raw%d%d" % (g, a), [P, 4, 256], F32) for a in two] for g in two]
-        slope = [[sbt("slope%d%d" % (g, a), [P, 4, 256], F32) for a in two] for g in two]
-        gd = [[sbt("gd%d%d" % (g, a), [P, 4, 256], F32) for a in two] for g in two]
+        y_raw = [[sbt("y_raw%d%d" % (g, a), [P, 1024], F32) for a in two] for g in two]
+        slope = [sbt("slope%d" % g, [P, 2048], F32) for g in two]
+        gd = [sbt("gd%d" % g, [P, 2048], F32) for g in two]
         z_il = [sbt("z_il%d" % g, [P, 2048], BF16) for g in two]
         z_c = [sbt("z_c%d" % g, [P, 512], U32) for g in two]
         z_s = [sbt("z_s%d" % g, [P, 512], U8) for g in two]
-        a_raw = [[sbt("a_raw%d%d" % (g, h), [P, 4, 512], BF16) for h in two] for g in two]
+        a_raw = [sbt("a_raw%d" % g, [P, 4, 1024], BF16) for g in two]
         a_il = [[sbt("a_il%d%d" % (g, h), [P, 2048], BF16) for h in two] for g in two]
         a_c = [[sbt("a_c%d%d" % (g, h), [P, 512], U32) for h in two] for g in two]
         a_s = [[sbt("a_s%d%d" % (g, h), [P, 512], U8) for h in two] for g in two]
@@ -95,25 +94,27 @@ def tile_gcnlayer_pb_v_kernel(tc, A1, Hn, Wout, bout, d, y, grad_out, out_0, out
             nc.tensor.matmul_mx(out=out, lhsT=lc.bitcast(lf), lhsT_scale=ls, rhs=rc.bitcast(rf), rhs_scale=rs, start=start, stop=stop)
 
         def a_views(g, h):
-            src = a_raw[g][h][:].rearrange("p j (mm m t) -> p mm t j m", m=2, t=4)
+            src = a_raw[g][:, :, 512 * h : 512 * (h + 1)].rearrange("p j (mm m t) -> p mm t m j", m=2, t=4)
             return src
 
         def step(name, eng):
             kind = name[:2]
             if name == "Id":
-                make_identity(nc, ident_g[:])
+                nc.vector.memset(ident_g[:], 0.0)
                 nc.scalar.activation(out=ident[:], in_=ident_g[:], func=ACT.Copy)
+                make_identity(nc, ident[:], nomemset=True)
             elif name == "Ld":
-                nc.scalar.dma_start(out=d_sb[:], in_=d.rearrange("(g p j) -> p g j", g=2, j=4))
+                for g in two:
+                    nc.scalar.dma_start(out=d_sb[g][:], in_=d[512 * g : 512 * (g + 1)].rearrange("(p j) -> p j", j=4))
             elif kind == "Lg":
                 g = int(name[2])
                 nc.sync.dma_start(out=g_raw[g][:], in_=rows(grad_out, g))
             elif kind == "Ly":
-                g, a = int(name[2]), "ab".index(name[3])
-                nc.sync.dma_start(out=y_raw[g][a][:], in_=rows(y, g)[:, :, 256 * a : 256 * (a + 1)])
+                g, a = int(name[2]), "pq".index(name[3])
+                nc.sync.dma_start(out=y_raw[g][a][:], in_=y[512 * g : 512 * (g + 1), :].rearrange("(p j) w -> p (j w)", j=4)[:, 1024 * a : 1024 * (a + 1)])
             elif kind == "LA":
-                g, h = int(name[2]), int(name[3])
-                nc.sync.dma_start(out=a_raw[g][h][:], in_=rows(A1, g)[:, :, 512 * h : 512 * (h + 1)])
+                g = int(name[2])
+                nc.sync.dma_start(out=a_raw[g][:], in_=rows(A1, g))
             elif kind == "LW":
                 nc.sync.dma_start(out=w_raw[:], in_=Wout.rearrange("(p a) o -> p (a o)", a=4))
             elif kind == "LH":
@@ -121,17 +122,17 @@ def tile_gcnlayer_pb_v_kernel(tc, A1, Hn, Wout, bout, d, y, grad_out, out_0, out
                 nc.sync.dma_start(out=h_raw[:, h], in_=rows(Hn, h))
             elif kind == "gd":
                 g, a = int(name[2]), "ab".index(name[3])
-                for j in four:
-                    nc.scalar.activation(out=gd[g][a][:, j, :], in_=g_raw[g][:, j, 256 * a : 256 * (a + 1)], func=ACT.Copy, scale=d_sb[:, g, j : j + 1])
+                for j in (2 * a, 2 * a + 1):
+                    nc.scalar.activation(out=gd[g][:, 512 * j : 512 * (j + 1)], in_=g_raw[g][:, j, :], func=ACT.Copy, scale=d_sb[g][:, j : j + 1])
             elif kind == "sl":
                 g, a = int(name[2]), "ab".index(name[3])
-                nc.vector.tensor_scalar(out=slope[g][a][:].rearrange("p j w -> p (j w)"), in0=y_raw[g][a][:].rearrange("p j w -> p (j w)"), scalar1=0.0, scalar2=SLOPE, op0=ALU.is_ge, op1=ALU.max)
+                nc.vector.tensor_scalar(out=slope[g][:, 1024 * a : 1024 * (a + 1)], in0=y_raw[g][a][:], scalar1=0.0, scalar2=SLOPE, op0=ALU.is_ge, op1=ALU.max)
             elif kind == "tt":
                 g, a = int(name[2]), "ab".index(name[3])
                 nc.vector.tensor_tensor(
                     out=z_il[g][:, 1024 * a : 1024 * (a + 1)].rearrange("p (c i j) -> p c j i", i=4, j=4),
-                    in0=gd[g][a][:].rearrange("p j (c i) -> p c j i", i=4),
-                    in1=slope[g][a][:].rearrange("p j (c i) -> p c j i", i=4),
+                    in0=gd[g][:].rearrange("p (j c i) -> p c j i", j=4, i=4)[:, 64 * a : 64 * (a + 1)],
+                    in1=slope[g][:].rearrange("p (j c i) -> p c j i", j=4, i=4)[:, 64 * a : 64 * (a + 1)],
                     op=ALU.mult,
                 )
             elif kind == "qz":
@@ -139,10 +140,10 @@ def tile_gcnlayer_pb_v_kernel(tc, A1, Hn, Wout, bout, d, y, grad_out, out_0, out
                 quant(z_c[g][:, 256 * a : 256 * (a + 1)], z_s[g][:, 256 * a : 256 * (a + 1)], z_il[g][:, 1024 * a : 1024 * (a + 1)], E5)
             elif kind == "iA":
                 g, h = int(name[2]), int(name[3])
-                copy(eng, a_il[g][h][:].rearrange("p (t mm m j) -> p mm t j m", t=4, m=2, j=4), a_views(g, h))
+                copy(eng, a_il[g][h][:].rearrange("p (t mm m j) -> p mm t m j", t=4, m=2, j=4), a_views(g, h))
             elif kind == "jA":
                 g, h, k = int(name[2]), int(name[3]), "ab".index(name[4])
-                copy(eng, a_il[g][h][:, 1024 * k : 1024 * (k + 1)].rearrange("p (t mm m j) -> p mm t j m", t=2, m=2, j=4), a_views(g, h)[:, :, 2 * k : 2 * k + 2])
+                copy(eng, a_il[g][h][:, 1024 * k : 1024 * (k + 1)].rearrange("p (t mm m j) -> p mm t m j", t=2, m=2, j=4), a_views(g, h)[:, :, 2 * k : 2 * k + 2])
             elif kind == "qA":
                 g, h = int(name[2]), int(name[3])
                 quant(a_c[g][h][:], a_s[g][h][:], a_il[g][h][:], E4)
@@ -170,9 +171,9 @@ def tile_gcnlayer_pb_v_kernel(tc, A1, Hn, Wout, bout, d, y, grad_out, out_0, out
                 dst = dz1[h][:, 512 * t : 512 * (t + 1)].rearrange("p (u m e) -> p u m e", u=2, e=2)
                 src = banks["dh%d%d" % (h, t)][:].rearrange("p (m u e) -> p u m e", u=2, e=2)
                 if eng == "S":
-                    nc.scalar.activation(out=dst, in_=src, func=ACT.Copy, scale=d_sb[:, h, t : t + 1])
+                    nc.scalar.activation(out=dst, in_=src, func=ACT.Copy, scale=d_sb[h][:, t : t + 1])
                 else:
-                    nc.vector.tensor_scalar(out=dst, in0=src, scalar1=d_sb[:, h, t : t + 1], scalar2=None, op0=ALU.mult)
+                    nc.vector.tensor_scalar(out=dst, in0=src, scalar1=d_sb[h][:, t : t + 1], scalar2=None, op0=ALU.mult)
             elif kind == "tF":
                 h, k = int(name[2]), "ab".index(name[3])
                 b = bank(name)

@@ -18,12 +18,13 @@ ALU = mybir.AluOpType
 ACT = mybir.ActivationFunctionType
 
 P = 128
-ORDER = """Ld Lg0 Ly0p Ly0q Lg1 LA0 Ly1p Ly1q LA1 LW LH0 LH1 Id
-gd0a gd0b sl0a sl0b tt0a tt0b qz0a gd1a gd1b jA00a@S qz0b jA00b@V iA01@S sl1a qA00 sl1b tt1a tt1b jA10a@S qz1a jA10b@V qz1b qA10
-d000 d001 d002 d003 tWa tWb jA11a@S cWa@S cWb@S d100 d101 d102 d103 jA11b@V qA01 qA11 Z00@S  Z01@S d010 d110 tF0a Z02@S Z03@S d011 d111 tF0b d012 d112 
-qW iH0@V iH1@V qH0 cF0a@S qH1 iH2@V qF0a d013 d113 o00 o01 iT0@V Z10@S cF0b@S Z11@S qF0b qT0
+ORDER = """Ld Lg0 Ly0p Ly0q Lg1 LA00 Ly1p Ly1q LA10 LA01 LW LA11 LH0 LH1 Id
+gd0a gd0b sl0a sl0b tt0a tt0b qz0a gd1a gd1b jA00a@S jA00b@V sl1a qz0b sl1b qA00 tt1a tt1b qz1a iA10@S 
+d000 d001 d002 d003 tWa tWb iA01@S cWa@S cWb@S qz1b qA10   
+d100 d101 d102 d103 iA11@V Z00@S qA01 Z01@S qA11 d010 d110 tF0a  Z02@S Z03@S d011 d111 tF0b d012 d112 
+qW iH0@V iH1@V qH0 cF0a@S qH1 qF0a d013 d113 o00 o01 iT0@V Z10@S cF0b@S Z11@S qF0b qT0
  tF1a o02 o03  Z12@S Z13@S E00@V S00 E01@V S01  tF1b w00 w01 cF1a@S qF1a o10 o11 iT1@V E02@S S02 cF1b@S  qF1b qT1 E03@S S03 
- o12 o13 w10 w11  iH3@V qH2 E10@S S10 E11@S S11 qH3 w02 w12 w03 w13 E12@S S12  E13@S S13 G0@S R0 G1@V R1 
+ o12 o13 w10 w11  iH2@V iH3@V qH2 E10@S S10 E11@S S11 qH3 w02 w12 w03 w13 E12@S S12  E13@S S13 G0@S R0 G1@V R1 
  G2@S R2 G3@V R3""".split()
 BANK = {"dh00":0,"dh01":1,"dh02":2,"dh03":3,"dh10":4,"dh11":5,"tWa":6,"tWb":7,"dh12":6,"dh13":7,"tF0a":0,"tF0b":1,"o00":2,"o01":3,"o02":0,"o03":1,"tF1a":4,"tF1b":5,"w0":6,"w1":7,"o10":2,"o11":3,"o12":4,"o13":0,"w2":5,"w3":1}
 
@@ -60,7 +61,7 @@ def tile_gcnlayer_pb_v_kernel(tc, A1, Hn, Wout, bout, d, y, grad_out, out_0, out
         z_il = [sbt("z_il%d" % g, [P, 2048], BF16) for g in two]
         z_c = [sbt("z_c%d" % g, [P, 512], U32) for g in two]
         z_s = [sbt("z_s%d" % g, [P, 512], U8) for g in two]
-        a_raw = [sbt("a_raw%d" % g, [P, 4, 1024], BF16) for g in two]
+        a_raw = [[sbt("a_raw%d%d" % (g, h), [P, 4, 512], BF16) for h in two] for g in two]
         a_il = [[sbt("a_il%d%d" % (g, h), [P, 2048], BF16) for h in two] for g in two]
         a_c = [[sbt("a_c%d%d" % (g, h), [P, 512], U32) for h in two] for g in two]
         a_s = [[sbt("a_s%d%d" % (g, h), [P, 512], U8) for h in two] for g in two]
@@ -94,7 +95,7 @@ def tile_gcnlayer_pb_v_kernel(tc, A1, Hn, Wout, bout, d, y, grad_out, out_0, out
             nc.tensor.matmul_mx(out=out, lhsT=lc.bitcast(lf), lhsT_scale=ls, rhs=rc.bitcast(rf), rhs_scale=rs, start=start, stop=stop)
 
         def a_views(g, h):
-            src = a_raw[g][:, :, 512 * h : 512 * (h + 1)].rearrange("p j (mm m t) -> p mm t m j", m=2, t=4)
+            src = a_raw[g][h][:].rearrange("p j (mm m t) -> p mm t m j", m=2, t=4)
             return src
 
         def step(name, eng):
@@ -113,8 +114,8 @@ def tile_gcnlayer_pb_v_kernel(tc, A1, Hn, Wout, bout, d, y, grad_out, out_0, out
                 g, a = int(name[2]), "pq".index(name[3])
                 nc.sync.dma_start(out=y_raw[g][a][:], in_=y[512 * g : 512 * (g + 1), :].rearrange("(p j) w -> p (j w)", j=4)[:, 1024 * a : 1024 * (a + 1)])
             elif kind == "LA":
-                g = int(name[2])
-                nc.sync.dma_start(out=a_raw[g][:], in_=rows(A1, g))
+                g, h = int(name[2]), int(name[3])
+                nc.sync.dma_start(out=a_raw[g][h][:], in_=rows(A1, g)[:, :, 512 * h : 512 * (h + 1)])
             elif kind == "LW":
                 nc.sync.dma_start(out=w_raw[:], in_=Wout.rearrange("(p a) o -> p (a o)", a=4))
             elif kind == "LH":
@@ -130,9 +131,9 @@ def tile_gcnlayer_pb_v_kernel(tc, A1, Hn, Wout, bout, d, y, grad_out, out_0, out
             elif kind == "tt":
                 g, a = int(name[2]), "ab".index(name[3])
                 nc.vector.tensor_tensor(
-                    out=z_il[g][:, 1024 * a : 1024 * (a + 1)].rearrange("p (c i j) -> p c j i", i=4, j=4),
-                    in0=gd[g][:].rearrange("p (j c i) -> p c j i", j=4, i=4)[:, 64 * a : 64 * (a + 1)],
-                    in1=slope[g][:].rearrange("p (j c i) -> p c j i", j=4, i=4)[:, 64 * a : 64 * (a + 1)],
+                    out=z_il[g][:, 1024 * a : 1024 * (a + 1)].rearrange("p (c i j) -> p c j i", i=2, j=4),
+                    in0=gd[g][:].rearrange("p (j c i) -> p c j i", j=4, i=2)[:, 128 * a : 128 * (a + 1)],
+                    in1=slope[g][:].rearrange("p (j c i) -> p c j i", j=4, i=2)[:, 128 * a : 128 * (a + 1)],
                     op=ALU.mult,
                 )
             elif kind == "qz":

from contextlib import ExitStack

import concourse.mybir as mybir
from concourse.masks import make_identity

N, D, O = 1024, 512, 512
SLOPE = 0.01
FLOPS = 2 * (N * N * O + 2 * N * O * D)
BYTES = 2 * (N * N + N * D + D * O + N * O) + 4 * (N + N * O) + 4 * (N * D + D * O)

F32 = mybir.dt.float32
BF16 = mybir.dt.bfloat16
U32 = mybir.dt.uint32
U8 = mybir.dt.uint8
E4 = mybir.dt.float8_e4m3fn_x4
E5 = mybir.dt.float8_e5m2_x4
ALU = mybir.AluOpType
ACT = mybir.ActivationFunctionType

P = 128
ORDER = """Ld Lg0 Ly0p Ly0q Lg1 LA00 Ly1p Ly1q LA10 LA01 LW LA11 LH0 LH1 Id
gd0a gd0b sl0a sl0b tt0a tt0b qz0a gd1a gd1b jA00a@S jA00b@V sl1a qz0b sl1b qA00 tt1a tt1b qz1a iA10@S 
d000 d001 d002 d003 tWa tWb iA01@S cWa@S cWb@S qz1b qA10   
d100 d101 d102 d103 iA11@V Z00@S qA01 Z01@S qA11 d010 d110 tF0a  Z02@S Z03@S d011 d111 tF0b d012 d112 
qW iH0@V iH1@V qH0 cF0a@S qH1 qF0a d013 d113 o00 o01 iT0@V Z10@S cF0b@S Z11@S qF0b qT0
 tF1a o02 o03  Z12@S Z13@S E00@V S00 E01@V S01  tF1b w00 w01 cF1a@S qF1a o10 o11 iT1@V E02@S S02 cF1b@S  qF1b qT1 E03@S S03 
 o12 o13 w10 w11  iH2@V iH3@V qH2 E10@S S10 E11@S S11 qH3 w02 w12 w03 w13 E12@S S12  E13@S S13 G0@S R0 G1@V R1 
 G2@S R2 G3@V R3""".split()
BANK = {"dh00":0,"dh01":1,"dh02":2,"dh03":3,"dh10":4,"dh11":5,"tWa":6,"tWb":7,"dh12":6,"dh13":7,"tF0a":0,"tF0b":1,"o00":2,"o01":3,"o02":0,"o03":1,"tF1a":4,"tF1b":5,"w0":6,"w1":7,"o10":2,"o11":3,"o12":4,"o13":0,"w2":5,"w3":1}


def tile_gcnlayer_pb_v_kernel(tc, A1, Hn, Wout, bout, d, y, grad_out, out_0, out_1):
    nc = tc.nc
    with ExitStack() as ctx:
        sb = ctx.enter_context(tc.tile_pool(name="sb", bufs=1))
        ps = ctx.enter_context(tc.psum_pool(name="ps", bufs=1))
        ctx.enter_context(tc.manual_schedule())

        def sbt(name, shape, dtype):
            return sb.tile(shape, dtype, name=name, tag=name, align_bytes=64)

        banks = {}

        def bank(name):
            banks[name] = ps.tile([P, 512], F32, name="ps_" + name, tag="bank%d" % BANK[name])
            return banks[name]

        def copy(eng, out, in_):
            if eng == "V":
                nc.vector.tensor_copy(out=out, in_=in_)
            else:
                nc.scalar.copy(out=out, in_=in_)

        two = (0, 1)
        four = (0, 1, 2, 3)
        d_sb = [sbt("d_sb%d" % g, [P, 4], F32) for g in two]
        g_raw = [sbt("g_raw%d" % g, [P, 4, 512], BF16) for g in two]
        y_raw = [[sbt("y_raw%d%d" % (g, a), [P, 1024], F32) for a in two] for g in two]
        slope = [sbt("slope%d" % g, [P, 2048], F32) for g in two]
        gd = [sbt("gd%d" % g, [P, 2048], F32) for g in two]
        z_il = [sbt("z_il%d" % g, [P, 2048], BF16) for g in two]
        z_c = [sbt("z_c%d" % g, [P, 512], U32) for g in two]
        z_s = [sbt("z_s%d" % g, [P, 512], U8) for g in two]
        a_raw = [[sbt("a_raw%d%d" % (g, h), [P, 4, 512], BF16) for h in two] for g in two]
        a_il = [[sbt("a_il%d%d" % (g, h), [P, 2048], BF16) for h in two] for g in two]
        a_c = [[sbt("a_c%d%d" % (g, h), [P, 512], U32) for h in two] for g in two]
        a_s = [[sbt("a_s%d%d" % (g, h), [P, 512], U8) for h in two] for g in two]
        w_raw = sbt("w_raw", [P, 2048], BF16)
        w_il = sbt("w_il", [P, 2048], BF16)
        w_c = sbt("w_c", [P, 512], U32)
        w_s = sbt("w_s", [P, 512], U8)
        h_raw = sbt("h_raw", [P, 2, 4, 512], BF16)
        h_il = [sbt("h_il%d" % a, [P, 1024], BF16) for a in four]
        h_c = [sbt("h_c%d" % a, [P, 256], U32) for a in four]
        h_s = [sbt("h_s%d" % a, [P, 256], U8) for a in four]
        dz1 = [sbt("dz1_%d" % h, [P, 2048], BF16) for h in two]
        f_il = [[sbt("f_il%d%d" % (h, k), [P, 1024], BF16) for k in two] for h in two]
        f_c = [[sbt("f_c%d%d" % (h, k), [P, 256], U32) for k in two] for h in two]
        f_s = [[sbt("f_s%d%d" % (h, k), [P, 256], U8) for k in two] for h in two]
        t_il = [sbt("t_il%d" % h, [P, 2048], BF16) for h in two]
        t_c = [sbt("t_c%d" % h, [P, 512], U32) for h in two]
        t_s = [sbt("t_s%d" % h, [P, 512], U8) for h in two]
        o0 = [[sbt("o0_%d%d" % (h, t), [P, 512], F32) for t in four] for h in two]
        o1 = [sbt("o1_%d" % a, [P, 512], F32) for a in four]
        ident_g = sbt("ident_g", [P, P], F32)
        ident = sbt("ident", [P, P], F32)

        def rows(src, g):
            return src[512 * g : 512 * (g + 1), :].rearrange("(p j) w -> p j w", j=4)

        def quant(codes, scales, src, fmt):
            nc.vector.quantize_mx(out=codes.bitcast(fmt), scales=scales, in_=src)

        def mm(out, lc, ls, lf, rc, rs, rf, start, stop):
            nc.tensor.matmul_mx(out=out, lhsT=lc.bitcast(lf), lhsT_scale=ls, rhs=rc.bitcast(rf), rhs_scale=rs, start=start, stop=stop)

        def a_views(g, h):
            src = a_raw[g][h][:].rearrange("p j (mm m t) -> p mm t m j", m=2, t=4)
            return src

        def step(name, eng):
            kind = name[:2]
            if name == "Id":
                nc.vector.memset(ident_g[:], 0.0)
                nc.scalar.activation(out=ident[:], in_=ident_g[:], func=ACT.Copy)
                make_identity(nc, ident[:], nomemset=True)
            elif name == "Ld":
                for g in two:
                    nc.scalar.dma_start(out=d_sb[g][:], in_=d[512 * g : 512 * (g + 1)].rearrange("(p j) -> p j", j=4))
            elif kind == "Lg":
                g = int(name[2])
                nc.sync.dma_start(out=g_raw[g][:], in_=rows(grad_out, g))
            elif kind == "Ly":
                g, a = int(name[2]), "pq".index(name[3])
                nc.sync.dma_start(out=y_raw[g][a][:], in_=y[512 * g : 512 * (g + 1), :].rearrange("(p j) w -> p (j w)", j=4)[:, 1024 * a : 1024 * (a + 1)])
            elif kind == "LA":
                g, h = int(name[2]), int(name[3])
                nc.sync.dma_start(out=a_raw[g][h][:], in_=rows(A1, g)[:, :, 512 * h : 512 * (h + 1)])
            elif kind == "LW":
                nc.sync.dma_start(out=w_raw[:], in_=Wout.rearrange("(p a) o -> p (a o)", a=4))
            elif kind == "LH":
                h = int(name[2])
                nc.sync.dma_start(out=h_raw[:, h], in_=rows(Hn, h))
            elif kind == "gd":
                g, a = int(name[2]), "ab".index(name[3])
                for j in (2 * a, 2 * a + 1):
                    nc.scalar.activation(out=gd[g][:, 512 * j : 512 * (j + 1)], in_=g_raw[g][:, j, :], func=ACT.Copy, scale=d_sb[g][:, j : j + 1])
            elif kind == "sl":
                g, a = int(name[2]), "ab".index(name[3])
                nc.vector.tensor_scalar(out=slope[g][:, 1024 * a : 1024 * (a + 1)], in0=y_raw[g][a][:], scalar1=0.0, scalar2=SLOPE, op0=ALU.is_ge, op1=ALU.max)
            elif kind == "tt":
                g, a = int(name[2]), "ab".index(name[3])
                nc.vector.tensor_tensor(
                    out=z_il[g][:, 1024 * a : 1024 * (a + 1)].rearrange("p (c i j) -> p c j i", i=2, j=4),
                    in0=gd[g][:].rearrange("p (j c i) -> p c j i", j=4, i=2)[:, 128 * a : 128 * (a + 1)],
                    in1=slope[g][:].rearrange("p (j c i) -> p c j i", j=4, i=2)[:, 128 * a : 128 * (a + 1)],
                    op=ALU.mult,
                )
            elif kind == "qz":
                g, a = int(name[2]), "ab".index(name[3])
                quant(z_c[g][:, 256 * a : 256 * (a + 1)], z_s[g][:, 256 * a : 256 * (a + 1)], z_il[g][:, 1024 * a : 1024 * (a + 1)], E5)
            elif kind == "iA":
                g, h = int(name[2]), int(name[3])
                copy(eng, a_il[g][h][:].rearrange("p (t mm m j) -> p mm t m j", t=4, m=2, j=4), a_views(g, h))
            elif kind == "jA":
                g, h, k = int(name[2]), int(name[3]), "ab".index(name[4])
                copy(eng, a_il[g][h][:, 1024 * k : 1024 * (k + 1)].rearrange("p (t mm m j) -> p mm t m j", t=2, m=2, j=4), a_views(g, h)[:, :, 2 * k : 2 * k + 2])
            elif kind == "qA":
                g, h = int(name[2]), int(name[3])
                quant(a_c[g][h][:], a_s[g][h][:], a_il[g][h][:], E4)
            elif kind == "tW":
                k = "ab".index(name[2])
                b = bank(name)
                words = w_raw[:].bitcast(F32)
                for a2 in two:
                    for u in two:
                        a = 2 * k + a2
                        nc.tensor.transpose(b[:, 128 * (2 * a2 + u) : 128 * (2 * a2 + u + 1)], words[:, 256 * a + u : 256 * (a + 1) : 2], ident[:])
            elif kind == "cW":
                k = "ab".index(name[2])
                copy(eng, w_il[:].bitcast(F32).rearrange("q (p a u) -> q p a u", a=4, u=2)[:, :, 2 * k : 2 * k + 2, :], banks["tW" + name[2]][:].rearrange("q (a u p) -> q p a u", a=2, u=2))
            elif name == "qW":
                quant(w_c[:], w_s[:], w_il[:], E4)
            elif name[0] == "d":
                g, h, t = int(name[1]), int(name[2]), int(name[3])
                key = "dh%d%d" % (h, t)
                b = bank(key) if g == 0 else banks[key]
                cols = slice(128 * t, 128 * (t + 1))
                mm(b[:], a_c[g][h][:, cols], a_s[g][h][:, cols], E4, z_c[g][:], z_s[g][:], E5, g == 0, g == 1)
            elif name[0] == "Z":
                h, t = int(name[1]), int(name[2])
                dst = dz1[h][:, 512 * t : 512 * (t + 1)].rearrange("p (u m e) -> p u m e", u=2, e=2)
                src = banks["dh%d%d" % (h, t)][:].rearrange("p (m u e) -> p u m e", u=2, e=2)
                if eng == "S":
                    nc.scalar.activation(out=dst, in_=src, func=ACT.Copy, scale=d_sb[h][:, t : t + 1])
                else:
                    nc.vector.tensor_scalar(out=dst, in0=src, scalar1=d_sb[h][:, t : t + 1], scalar2=None, op0=ALU.mult)
            elif kind == "tF":
                h, k = int(name[2]), "ab".index(name[3])
                b = bank(name)
                for t2 in two:
                    for u in two:
                        c0 = 512 * (2 * k + t2) + 256 * u
                        nc.tensor.transpose(b[:, 128 * (2 * t2 + u) : 128 * (2 * t2 + u + 1)], dz1[h][:, c0 : c0 + 256].bitcast(F32), ident[:])
            elif kind == "cF":
                h, k = int(name[2]), "ab".index(name[3])
                copy(eng, f_il[h][k][:].bitcast(F32).rearrange("p (t r u) -> p t r u", t=2, u=2), banks["tF" + name[2:]][:].rearrange("p (t u r) -> p t r u", t=2, u=2))
            elif kind == "qF":
                h, k = int(name[2]), "ab".index(name[3])
                quant(f_c[h][k][:], f_s[h][k][:], f_il[h][k][:], E5)
            elif kind == "iT":
                h = int(name[2])
                copy(eng, t_il[h][:].rearrange("p (c i t) -> p c t i", i=4, t=4), dz1[h][:].rearrange("p (t c i) -> p c t i", i=4, t=4))
            elif kind == "qT":
                h = int(name[2])
                quant(t_c[h][:], t_s[h][:], t_il[h][:], E5)
            elif kind == "iH":
                a = int(name[2])
                copy(eng, h_il[a][:].rearrange("p (h c i j) -> p h c j i", h=2, i=4, j=4), h_raw[:, :, :, 128 * a : 128 * (a + 1)].rearrange("p h j (c i) -> p h c j i", i=4))
            elif kind == "qH":
                a = int(name[2])
                quant(h_c[a][:], h_s[a][:], h_il[a][:], E4)
            elif name[0] == "o":
                h, t = int(name[1]), int(name[2])
                b = bank(name)
                cols = slice(128 * (t % 2), 128 * (t % 2 + 1))
                mm(b[:], f_c[h][t // 2][:, cols], f_s[h][t // 2][:, cols], E5, w_c[:], w_s[:], E4, True, True)
            elif name[0] == "w":
                h, a = int(name[1]), int(name[2])
                key = "w%d" % a
                b = bank(key) if h == 0 else banks[key]
                cols = slice(128 * h, 128 * (h + 1))
                mm(b[:], h_c[a][:, cols], h_s[a][:, cols], E4, t_c[h][:], t_s[h][:], E5, h == 0, h == 1)
            elif name[0] == "E":
                h, t = int(name[1]), int(name[2])
                copy(eng, o0[h][t][:], banks["o%d%d" % (h, t)][:])
            elif name[0] == "S":
                h, t = int(name[1]), int(name[2])
                nc.sync.dma_start(out=out_0[512 * h : 512 * (h + 1), :].rearrange("(p t) w -> p t w", t=4)[:, t, :], in_=o0[h][t][:])
            elif name[0] == "G":
                a = int(name[1])
                copy(eng, o1[a][:].rearrange("p (m u e) -> p m u e", u=2, e=2), banks["w%d" % a][:].rearrange("p (u m e) -> p m u e", u=2, e=2))
            elif name[0] == "R":
                a = int(name[1])
                nc.sync.dma_start(out=out_1[128 * a : 128 * (a + 1), :], in_=o1[a][:])
            else:
                raise ValueError(name)

        for item in ORDER:
            parts = item.split("@")
            step(parts[0], parts[1] if len(parts) > 1 else "")
